import numpy as np
import ml_dtypes


def mxq(x, axis, fmt="e4m3"):
    dtype, down = {"e4m3": (ml_dtypes.float8_e4m3fn, 7), "e5m2": (ml_dtypes.float8_e5m2, 14)}[fmt]
    v = np.moveaxis(np.asarray(x, np.float32).astype(ml_dtypes.bfloat16).astype(np.float64), axis, -1)
    blocks = v.reshape(v.shape[:-1] + (-1, 32))
    amax = np.abs(blocks).max(-1, keepdims=True)
    byte = np.maximum(np.where(amax > 0, np.frexp(amax)[1] - 1 + 127, 0) - down, 1)
    scale = np.exp2(byte - 127.0)
    codes = (blocks / scale).astype(np.float32).astype(dtype).astype(np.float64)
    return np.moveaxis((codes * scale).reshape(v.shape), -1, axis)


WIDE = False


def mx_kscale(k):
    if not WIDE:
        return np.ones(k)
    levels = np.array([10, -10, 5, -5, 0])
    a = np.random.permutation(np.resize(levels, k // 512 * 4)).reshape(k // 512, 4)
    idx = np.arange(k)
    return np.exp2(a[idx // 512, idx % 128 // 32])


BF16 = ml_dtypes.bfloat16


def bf(x):
    return np.asarray(x, np.float32).astype(BF16)


def f64(x):
    return np.asarray(x).astype(np.float64)


B, D, H = 512, 1024, 1024
QH = True


def sigmoid(v):
    return 1.0 / (1.0 + np.exp(-v))


def xavier(rows, cols):
    limit = np.sqrt(6.0 / (rows + cols))
    return np.random.uniform(-limit, limit, (rows, cols))


def setup_inputs():
    s = mx_kscale(D)
    t = mx_kscale(H) if QH else np.ones(H)
    inp = {"x": bf(np.random.standard_normal((B, D)) * s), "h0": bf(np.random.standard_normal((B, H)) * t), "c0": bf(np.random.standard_normal((B, H)))}
    for n in ("i", "f", "g", "o"):
        inp["W_i" + n] = bf(xavier(H, D) / s)
        inp["b_i" + n] = bf(np.random.standard_normal(H) * 0.1)
        inp["W_h" + n] = bf(xavier(H, H) / t)
        inp["b_h" + n] = bf(np.random.standard_normal(H) * 0.1)
    return inp


def reference(x, h0, c0,
              W_ii, b_ii, W_hi, b_hi,
              W_if, b_if, W_hf, b_hf,
              W_ig, b_ig, W_hg, b_hg,
              W_io, b_io, W_ho, b_ho):
    Wx = np.concatenate([f64(W_ii), f64(W_if), f64(W_ig), f64(W_io)], axis=0)
    Wh = np.concatenate([f64(W_hi), f64(W_hf), f64(W_hg), f64(W_ho)], axis=0)
    b = np.concatenate([f64(b_ii) + f64(b_hi), f64(b_if) + f64(b_hf), f64(b_ig) + f64(b_hg), f64(b_io) + f64(b_ho)])
    gx = mxq(f64(x), 1, "e4m3") @ mxq(Wx, 1, "e4m3").T
    if QH:
        gh = mxq(f64(h0), 1, "e4m3") @ mxq(Wh, 1, "e4m3").T
    else:
        gh = f64(h0) @ Wh.T
    gates = gx + gh + b
    i_t = sigmoid(gates[:, 0 * H:1 * H])
    f_t = sigmoid(gates[:, 1 * H:2 * H])
    g_t = np.tanh(gates[:, 2 * H:3 * H])
    o_t = sigmoid(gates[:, 3 * H:4 * H])
    c_t = f_t * c0_f(c0) + i_t * g_t
    h_t = o_t * np.tanh(c_t)
    return (h_t, c_t)


def c0_f(c0):
    return f64(c0)

@@ -1,0 +1,263 @@
+from contextlib import ExitStack
+
+import concourse.mybir as mybir
+from concourse.masks import make_identity
+
+F32 = mybir.dt.float32
+BF16 = mybir.dt.bfloat16
+U32 = mybir.dt.uint32
+U8 = mybir.dt.uint8
+FP8X4 = mybir.dt.float8_e4m3fn_x4
+ACT = mybir.ActivationFunctionType
+ALU = mybir.AluOpType
+
+P = 128
+BATCH = 512
+K = 1024
+HID = 1024
+NT = HID // P
+FLOPS = 2 * BATCH * (2 * K) * (4 * HID)
+
+AHEAD = 5
+STORE_GROUPS = ((0, 1), (2, 3), (4, 5), (6,), (7,))
+W_EVAC_ON_SCALAR = (True, False, True, False, True, False, True, True)
+
+
+def tile_lstmcell_kernel(
+    tc, x, h0, c0,
+    W_ii, b_ii, W_hi, b_hi,
+    W_if, b_if, W_hf, b_hf,
+    W_ig, b_ig, W_hg, b_hg,
+    W_io, b_io, W_ho, b_ho,
+    out_0, out_1,
+):
+    nc = tc.nc
+    weights = ((W_ii, W_hi), (W_ig, W_hg), (W_if, W_hf), (W_io, W_ho))
+    biases = ((b_ii, b_hi), (b_ig, b_hg), (b_if, b_hf), (b_io, b_ho))
+    funcs = (ACT.Sigmoid, ACT.Tanh, ACT.Sigmoid, ACT.Sigmoid)
+    out_h = out_0.rearrange("(p t) h -> p t h", t=4)
+    out_c = out_1.rearrange("(p t) h -> p t h", t=4)
+
+    with ExitStack() as ctx:
+        const = ctx.enter_context(tc.tile_pool(name="const", bufs=1))
+        wraw_pool = ctx.enter_context(tc.tile_pool(name="wraw", bufs=8 * AHEAD))
+        grp_pool = ctx.enter_context(tc.tile_pool(name="grp", bufs=2))
+        code_pool = ctx.enter_context(tc.tile_pool(name="code", bufs=2))
+        act_pool = ctx.enter_context(tc.tile_pool(name="act", bufs=2))
+        ep_pool = ctx.enter_context(tc.tile_pool(name="ep", bufs=2))
+        out_pool = ctx.enter_context(tc.tile_pool(name="outp", bufs=2))
+        acc_pool = ctx.enter_context(tc.psum_pool(name="acc", bufs=1))
+        tr_pool = ctx.enter_context(tc.psum_pool(name="tr", bufs=4))
+        ctx.enter_context(tc.manual_schedule())
+
+        ident = const.tile([P, P], F32, name="ident")
+        make_identity(nc, ident[:])
+        warm = const.tile([P, 1], F32, name="warm")
+        nc.vector.memset(warm[:], 0.0)
+        braw = const.tile([P, 2 * P], BF16, name="braw")
+        nc.vector.memset(braw[:], 0.0)
+
+        xraw = []
+        for s, src in enumerate((x, h0)):
+            xr = const.tile([P, 4 * K], BF16, name="xraw%d" % s)
+            view = src.rearrange("(p t) k -> p t k", t=4)
+            for th in range(2):
+                nc.sync.dma_start(
+                    out=xr[:, th * 2 * K:(th + 1) * 2 * K].rearrange("p (t k) -> p t k", t=2),
+                    in_=view[:, 2 * th:2 * th + 2, :],
+                )
+            xraw.append(xr)
+        for q in range(4):
+            for s in range(2):
+                nc.scalar.dma_start(
+                    out=braw[8 * q:8 * q + 8, s * P:(s + 1) * P],
+                    in_=biases[q][s].rearrange("(j p) -> j p", p=P),
+                )
+        nc.scalar.activation(out=warm[:], in_=warm[:], func=ACT.Sigmoid)
+
+        wraw = {}
+
+        def load_weights(j):
+            tiles = []
+            for q in range(4):
+                for s in range(2):
+                    w = wraw_pool.tile([P, K], BF16, name="w%d_%d_%d" % (j, q, s), tag="w")
+                    nc.sync.dma_start(out=w[:], in_=weights[q][s][j * P:(j + 1) * P, :])
+                    tiles.append(w)
+            wraw[j] = tiles
+
+        load_weights(0)
+        load_weights(1)
+        c0_sb = const.tile([P, 4 * HID], BF16, name="c0_sb")
+        nc.sync.dma_start(out=c0_sb[:], in_=c0.rearrange("(p t) h -> p (t h)", t=4))
+        c0_v = c0_sb[:].rearrange("p (t h) -> p t h", t=4)
+        for j in range(2, AHEAD):
+            load_weights(j)
+
+        def transpose_bank(src32, cols, dst32, on_scalar, name):
+            bank = tr_pool.tile([P, 512], F32, name=name, tag="tr")
+            for i, c in enumerate(cols):
+                nc.tensor.transpose(bank[:, i * P:(i + 1) * P], src32[:, c:c + P], ident[:])
+            src = bank[:].rearrange("p (a u c) -> p a c u", a=2, u=2)
+            dst = dst32.rearrange("p (a c u) -> p a c u", a=2, u=2)
+            if on_scalar:
+                nc.scalar.copy(out=dst, in_=src)
+            else:
+                nc.vector.tensor_copy(out=dst, in_=src)
+
+        xq = const.tile([P, 4 * 512], U32, name="xq", align_bytes=64)
+        xs = const.tile([P, 4 * 512], U8, name="xs", align_bytes=64)
+        xgrp = grp_pool.tile([P, 8192], BF16, name="xgrp", tag="grp", align_bytes=64)
+        xgrp32 = xgrp[:].bitcast(F32)
+
+        def tr_x(s, th):
+            x32 = xraw[s][:].bitcast(F32)
+            for g in range(2):
+                cols = [(2 * th + tt) * 512 + 256 * g + 128 * u for tt in range(2) for u in range(2)]
+                base = (2 * s + g) * 1024 + th * 512
+                transpose_bank(x32, cols, xgrp32[:, base:base + 512], g == 0, "xb%d%d%d" % (s, th, g))
+
+        def quant_x(s):
+            nc.vector.quantize_mx(
+                out=xq[:, s * 1024:(s + 1) * 1024].bitcast(FP8X4),
+                scales=xs[:, s * 1024:(s + 1) * 1024],
+                in_=xgrp[:, s * 4096:(s + 1) * 4096],
+            )
+
+        tr_x(0, 0)
+        tr_x(0, 1)
+        tr_x(1, 0)
+        quant_x(0)
+        tr_x(1, 1)
+
+        bsum = const.tile([P, P], F32, name="bsum")
+        nc.vector.tensor_tensor(out=bsum[:], in0=braw[:, 0:P], in1=braw[:, P:2 * P], op=ALU.add)
+        pb = tr_pool.tile([P, 512], F32, name="pb", tag="tr")
+        nc.tensor.transpose(pb[:, 0:P], bsum[:], ident[:])
+        bias_sb = const.tile([P, 32], F32, name="bias_sb")
+        nc.vector.tensor_copy(out=bias_sb[:], in_=pb[:, 0:32])
+        quant_x(1)
+
+        grp = {}
+        wq = {}
+        ws = {}
+        gate = {}
+        prod = {}
+        banks = {}
+        outs = {}
+        tanh_c = {}
+
+        def tr_w(j, q):
+            if q == 0:
+                grp[j] = grp_pool.tile([P, 8192], BF16, name="grp%d" % j, tag="grp", align_bytes=64)
+            g32 = grp[j][:].bitcast(F32)
+            for s in range(2):
+                m = 2 * q + s
+                transpose_bank(
+                    wraw[j][m][:].bitcast(F32), (0, 128, 256, 384), g32[:, m * 512:(m + 1) * 512],
+                    W_EVAC_ON_SCALAR[m], "wb%d_%d" % (j, m),
+                )
+
+        def quant(j, q):
+            if q == 0:
+                wq[j] = code_pool.tile([P, 2048], U32, name="wq%d" % j, tag="wq", align_bytes=64)
+                ws[j] = code_pool.tile([P, 2048], U8, name="ws%d" % j, tag="ws", align_bytes=64)
+            nc.vector.quantize_mx(
+                out=wq[j][:, q * 512:(q + 1) * 512].bitcast(FP8X4),
+                scales=ws[j][:, q * 512:(q + 1) * 512],
+                in_=grp[j][:, q * 2048:(q + 1) * 2048],
+            )
+
+        def mx_act(j, q):
+            acc = acc_pool.tile([P, 512], F32, name="acc%d_%d" % (j, q), tag="acc%d" % q)
+            for s in range(2):
+                for g in range(2):
+                    wc = (2 * q + s) * 256 + g * 128
+                    xc = (2 * s + g) * 512
+                    nc.tensor.matmul_mx(
+                        out=acc[:],
+                        lhsT=wq[j][:, wc:wc + 128].bitcast(FP8X4),
+                        lhsT_scale=ws[j][:, wc:wc + 128],
+                        rhs=xq[:, xc:xc + 512].bitcast(FP8X4),
+                        rhs_scale=xs[:, xc:xc + 512],
+                        start=(s == 0 and g == 0),
+                        stop=(s == 1 and g == 1),
+                    )
+            a = act_pool.tile([P, 512], F32, name="gate%d_%d" % (j, q), tag="gate%d" % q)
+            nc.scalar.activation(
+                out=a[:], in_=acc[:], func=funcs[q],
+                bias=bias_sb[:, 8 * q + j:8 * q + j + 1], scale=1.0,
+            )
+            gate[(j, q)] = a
+
+        def mul_ig(j):
+            t = act_pool.tile([P, 512], F32, name="ig%d" % j, tag="ig")
+            nc.vector.tensor_tensor(out=t[:], in0=gate[(j, 0)][:], in1=gate[(j, 1)][:], op=ALU.mult)
+            prod[j] = t
+
+        def tr_out(j):
+            for key, src in (("f", gate[(j, 2)]), ("u", prod[j]), ("o", gate[(j, 3)])):
+                bank = tr_pool.tile([P, 512], F32, name="ob%s%d" % (key, j), tag="tr")
+                for t in range(4):
+                    nc.tensor.transpose(bank[:, t * P:(t + 1) * P], src[:, t * P:(t + 1) * P], ident[:])
+                banks[(j, key)] = bank[:].rearrange("p (t h) -> p t h", t=4)
+
+        def group_of(j):
+            for grp_js in STORE_GROUPS:
+                if j in grp_js:
+                    return grp_js
+            return None
+
+        def ep1(j):
+            js = group_of(j)
+            width = P * len(js)
+            if j == js[0]:
+                outs[js] = (
+                    out_pool.tile([P, 4, width], F32, name="oh%d" % j, tag="oh"),
+                    out_pool.tile([P, 4, width], F32, name="oc%d" % j, tag="oc"),
+                )
+            off = (j - js[0]) * P
+            oc_v = outs[js][1][:, :, off:off + P]
+            t1 = ep_pool.tile([P, 4, P], F32, name="t1_%d" % j, tag="t1")
+            nc.vector.tensor_tensor(out=t1[:], in0=banks[(j, "f")], in1=c0_v[:, :, j * P:(j + 1) * P], op=ALU.mult)
+            nc.vector.tensor_tensor(out=oc_v, in0=banks[(j, "u")], in1=t1[:], op=ALU.add)
+            th = ep_pool.tile([P, 4, P], F32, name="th%d" % j, tag="th")
+            nc.scalar.activation(out=th[:], in_=oc_v, func=ACT.Tanh)
+            tanh_c[j] = th
+            if j == js[-1]:
+                nc.sync.dma_start(out=out_c[:, :, js[0] * P:(js[-1] + 1) * P], in_=outs[js][1][:])
+
+        def ep2(j):
+            js = group_of(j)
+            off = (j - js[0]) * P
+            nc.vector.tensor_tensor(
+                out=outs[js][0][:, :, off:off + P], in0=banks[(j, "o")], in1=tanh_c[j][:], op=ALU.mult,
+            )
+            if j == js[-1]:
+                nc.sync.dma_start(out=out_h[:, :, js[0] * P:(js[-1] + 1) * P], in_=outs[js][0][:])
+
+        for j in range(NT):
+            tr_w(j, 0)
+            tr_w(j, 1)
+            quant(j, 0)
+            tr_w(j, 2)
+            quant(j, 1)
+            tr_w(j, 3)
+            if j + AHEAD < NT:
+                load_weights(j + AHEAD)
+            if j >= 1:
+                tr_out(j - 1)
+            quant(j, 2)
+            if j >= 1:
+                ep1(j - 1)
+            quant(j, 3)
+            mx_act(j, 0)
+            mx_act(j, 1)
+            if j >= 1:
+                ep2(j - 1)
+            mul_ig(j)
+            mx_act(j, 2)
+            mx_act(j, 3)
+        tr_out(NT - 1)
+        ep1(NT - 1)
+        ep2(NT - 1)

@@ -16,11 +16,14 @@ BATCH = 512
 K = 1024
 HID = 1024
 NT = HID // P
+NR = 2 * NT
 FLOPS = 2 * BATCH * (2 * K) * (4 * HID)
 
-AHEAD = 5
+AHEAD = 10
+C0_AFTER = 3
 STORE_GROUPS = ((0, 1), (2, 3), (4, 5), (6,), (7,))
-W_EVAC_ON_SCALAR = (True, False, True, False, True, False, True, True)
+W_EVAC_ON_SCALAR = (True, False, True, True)
+TAIL_PARTS = 2
 
 
 def tile_lstmcell_kernel(
@@ -40,14 +43,14 @@ def tile_lstmcell_kernel(
 
     with ExitStack() as ctx:
         const = ctx.enter_context(tc.tile_pool(name="const", bufs=1))
-        wraw_pool = ctx.enter_context(tc.tile_pool(name="wraw", bufs=8 * AHEAD))
-        grp_pool = ctx.enter_context(tc.tile_pool(name="grp", bufs=2))
-        code_pool = ctx.enter_context(tc.tile_pool(name="code", bufs=2))
+        wraw_pool = ctx.enter_context(tc.tile_pool(name="wraw", bufs=4 * AHEAD))
+        grp_pool = ctx.enter_context(tc.tile_pool(name="grp", bufs=3))
+        code_pool = ctx.enter_context(tc.tile_pool(name="code", bufs=3))
         act_pool = ctx.enter_context(tc.tile_pool(name="act", bufs=2))
         ep_pool = ctx.enter_context(tc.tile_pool(name="ep", bufs=2))
         out_pool = ctx.enter_context(tc.tile_pool(name="outp", bufs=2))
-        acc_pool = ctx.enter_context(tc.psum_pool(name="acc", bufs=1))
-        tr_pool = ctx.enter_context(tc.psum_pool(name="tr", bufs=4))
+        acc_pool = ctx.enter_context(tc.psum_pool(name="acc", bufs=2))
+        tr_pool = ctx.enter_context(tc.psum_pool(name="tr", bufs=6))
         ctx.enter_context(tc.manual_schedule())
 
         ident = const.tile([P, P], F32, name="ident")
@@ -75,24 +78,24 @@ def tile_lstmcell_kernel(
                 )
         nc.scalar.activation(out=warm[:], in_=warm[:], func=ACT.Sigmoid)
 
+        c0_sb = const.tile([P, 4 * HID], BF16, name="c0_sb")
+        c0_v = c0_sb[:].rearrange("p (t h) -> p t h", t=4)
         wraw = {}
 
-        def load_weights(j):
+        def load_round(r):
+            j = r // 2
             tiles = []
-            for q in range(4):
+            for hh in range(2):
                 for s in range(2):
-                    w = wraw_pool.tile([P, K], BF16, name="w%d_%d_%d" % (j, q, s), tag="w")
-                    nc.sync.dma_start(out=w[:], in_=weights[q][s][j * P:(j + 1) * P, :])
+                    w = wraw_pool.tile([P, K], BF16, name="w%d_%d_%d" % (r, hh, s), tag="w")
+                    nc.sync.dma_start(out=w[:], in_=weights[2 * (r % 2) + hh][s][j * P:(j + 1) * P, :])
                     tiles.append(w)
-            wraw[j] = tiles
+            wraw[r] = tiles
+            if r == C0_AFTER:
+                nc.sync.dma_start(out=c0_sb[:], in_=c0.rearrange("(p t) h -> p (t h)", t=4))
 
-        load_weights(0)
-        load_weights(1)
-        c0_sb = const.tile([P, 4 * HID], BF16, name="c0_sb")
-        nc.sync.dma_start(out=c0_sb[:], in_=c0.rearrange("(p t) h -> p (t h)", t=4))
-        c0_v = c0_sb[:].rearrange("p (t h) -> p t h", t=4)
-        for j in range(2, AHEAD):
-            load_weights(j)
+        for r in range(AHEAD):
+            load_round(r)
 
         def transpose_bank(src32, cols, dst32, on_scalar, name):
             bank = tr_pool.tile([P, 512], F32, name=name, tag="tr")
@@ -107,36 +110,25 @@ def tile_lstmcell_kernel(
 
         xq = const.tile([P, 4 * 512], U32, name="xq", align_bytes=64)
         xs = const.tile([P, 4 * 512], U8, name="xs", align_bytes=64)
-        xgrp = grp_pool.tile([P, 8192], BF16, name="xgrp", tag="grp", align_bytes=64)
-        xgrp32 = xgrp[:].bitcast(F32)
+        xgrp = []
+        for s in range(2):
+            xg = grp_pool.tile([P, 4096], BF16, name="xgrp%d" % s, tag="grp", align_bytes=64)
+            xgrp.append(xg)
 
         def tr_x(s, th):
             x32 = xraw[s][:].bitcast(F32)
+            g32 = xgrp[s][:].bitcast(F32)
             for g in range(2):
                 cols = [(2 * th + tt) * 512 + 256 * g + 128 * u for tt in range(2) for u in range(2)]
-                base = (2 * s + g) * 1024 + th * 512
-                transpose_bank(x32, cols, xgrp32[:, base:base + 512], g == 0, "xb%d%d%d" % (s, th, g))
+                base = g * 1024 + th * 512
+                transpose_bank(x32, cols, g32[:, base:base + 512], g == 0, "xb%d%d%d" % (s, th, g))
 
         def quant_x(s):
             nc.vector.quantize_mx(
                 out=xq[:, s * 1024:(s + 1) * 1024].bitcast(FP8X4),
                 scales=xs[:, s * 1024:(s + 1) * 1024],
-                in_=xgrp[:, s * 4096:(s + 1) * 4096],
+                in_=xgrp[s][:],
             )
-
-        tr_x(0, 0)
-        tr_x(0, 1)
-        tr_x(1, 0)
-        quant_x(0)
-        tr_x(1, 1)
-
-        bsum = const.tile([P, P], F32, name="bsum")
-        nc.vector.tensor_tensor(out=bsum[:], in0=braw[:, 0:P], in1=braw[:, P:2 * P], op=ALU.add)
-        pb = tr_pool.tile([P, 512], F32, name="pb", tag="tr")
-        nc.tensor.transpose(pb[:, 0:P], bsum[:], ident[:])
-        bias_sb = const.tile([P, 32], F32, name="bias_sb")
-        nc.vector.tensor_copy(out=bias_sb[:], in_=pb[:, 0:32])
-        quant_x(1)
 
         grp = {}
         wq = {}
@@ -147,37 +139,34 @@ def tile_lstmcell_kernel(
         outs = {}
         tanh_c = {}
 
-        def tr_w(j, q):
-            if q == 0:
-                grp[j] = grp_pool.tile([P, 8192], BF16, name="grp%d" % j, tag="grp", align_bytes=64)
-            g32 = grp[j][:].bitcast(F32)
-            for s in range(2):
-                m = 2 * q + s
+        def tr_w(r):
+            grp[r] = grp_pool.tile([P, 4096], BF16, name="grp%d" % r, tag="grp", align_bytes=64)
+            g32 = grp[r][:].bitcast(F32)
+            for m in range(4):
                 transpose_bank(
-                    wraw[j][m][:].bitcast(F32), (0, 128, 256, 384), g32[:, m * 512:(m + 1) * 512],
-                    W_EVAC_ON_SCALAR[m], "wb%d_%d" % (j, m),
+                    wraw[r][m][:].bitcast(F32), (0, 128, 256, 384), g32[:, m * 512:(m + 1) * 512],
+                    W_EVAC_ON_SCALAR[m], "wb%d_%d" % (r, m),
                 )
+            if r + AHEAD < NR:
+                load_round(r + AHEAD)
 
-        def quant(j, q):
-            if q == 0:
-                wq[j] = code_pool.tile([P, 2048], U32, name="wq%d" % j, tag="wq", align_bytes=64)
-                ws[j] = code_pool.tile([P, 2048], U8, name="ws%d" % j, tag="ws", align_bytes=64)
-            nc.vector.quantize_mx(
-                out=wq[j][:, q * 512:(q + 1) * 512].bitcast(FP8X4),
-                scales=ws[j][:, q * 512:(q + 1) * 512],
-                in_=grp[j][:, q * 2048:(q + 1) * 2048],
-            )
+        def quant(r):
+            wq[r] = code_pool.tile([P, 1024], U32, name="wq%d" % r, tag="wq", align_bytes=64)
+            ws[r] = code_pool.tile([P, 1024], U8, name="ws%d" % r, tag="ws", align_bytes=64)
+            nc.vector.quantize_mx(out=wq[r][:].bitcast(FP8X4), scales=ws[r][:], in_=grp[r][:])
 
-        def mx_act(j, q):
-            acc = acc_pool.tile([P, 512], F32, name="acc%d_%d" % (j, q), tag="acc%d" % q)
+        def mx_act(r, hh):
+            j = r // 2
+            q = 2 * (r % 2) + hh
+            acc = acc_pool.tile([P, 512], F32, name="acc%d_%d" % (j, q), tag="acc")
             for s in range(2):
                 for g in range(2):
-                    wc = (2 * q + s) * 256 + g * 128
+                    wc = (2 * hh + s) * 256 + g * 128
                     xc = (2 * s + g) * 512
                     nc.tensor.matmul_mx(
                         out=acc[:],
-                        lhsT=wq[j][:, wc:wc + 128].bitcast(FP8X4),
-                        lhsT_scale=ws[j][:, wc:wc + 128],
+                        lhsT=wq[r][:, wc:wc + 128].bitcast(FP8X4),
+                        lhsT_scale=ws[r][:, wc:wc + 128],
                         rhs=xq[:, xc:xc + 512].bitcast(FP8X4),
                         rhs_scale=xs[:, xc:xc + 512],
                         start=(s == 0 and g == 0),
@@ -195,12 +184,12 @@ def tile_lstmcell_kernel(
             nc.vector.tensor_tensor(out=t[:], in0=gate[(j, 0)][:], in1=gate[(j, 1)][:], op=ALU.mult)
             prod[j] = t
 
-        def tr_out(j):
-            for key, src in (("f", gate[(j, 2)]), ("u", prod[j]), ("o", gate[(j, 3)])):
-                bank = tr_pool.tile([P, 512], F32, name="ob%s%d" % (key, j), tag="tr")
-                for t in range(4):
-                    nc.tensor.transpose(bank[:, t * P:(t + 1) * P], src[:, t * P:(t + 1) * P], ident[:])
-                banks[(j, key)] = bank[:].rearrange("p (t h) -> p t h", t=4)
+        def tr_out(j, key):
+            src = {"f": gate[(j, 2)], "u": prod[j], "o": gate[(j, 3)]}[key]
+            bank = tr_pool.tile([P, 512], F32, name="ob%s%d" % (key, j), tag="tr")
+            for t in range(4):
+                nc.tensor.transpose(bank[:, t * P:(t + 1) * P], src[:, t * P:(t + 1) * P], ident[:])
+            banks[(j, key)] = bank[:].rearrange("p (t h) -> p t h", t=4)
 
         def group_of(j):
             for grp_js in STORE_GROUPS:
@@ -208,7 +197,7 @@ def tile_lstmcell_kernel(
                     return grp_js
             return None
 
-        def ep1(j):
+        def ep_c(j, parts):
             js = group_of(j)
             width = P * len(js)
             if j == js[0]:
@@ -217,47 +206,70 @@ def tile_lstmcell_kernel(
                     out_pool.tile([P, 4, width], F32, name="oc%d" % j, tag="oc"),
                 )
             off = (j - js[0]) * P
-            oc_v = outs[js][1][:, :, off:off + P]
             t1 = ep_pool.tile([P, 4, P], F32, name="t1_%d" % j, tag="t1")
-            nc.vector.tensor_tensor(out=t1[:], in0=banks[(j, "f")], in1=c0_v[:, :, j * P:(j + 1) * P], op=ALU.mult)
-            nc.vector.tensor_tensor(out=oc_v, in0=banks[(j, "u")], in1=t1[:], op=ALU.add)
             th = ep_pool.tile([P, 4, P], F32, name="th%d" % j, tag="th")
-            nc.scalar.activation(out=th[:], in_=oc_v, func=ACT.Tanh)
+            n = 4 // parts
+            for part in range(parts):
+                ts = slice(part * n, (part + 1) * n)
+                oc_v = outs[js][1][:, ts, off:off + P]
+                nc.vector.tensor_tensor(
+                    out=t1[:, ts, :], in0=banks[(j, "f")][:, ts, :], in1=c0_v[:, ts, j * P:(j + 1) * P], op=ALU.mult,
+                )
+                nc.vector.tensor_tensor(out=oc_v, in0=banks[(j, "u")][:, ts, :], in1=t1[:, ts, :], op=ALU.add)
+                nc.scalar.activation(out=th[:, ts, :], in_=oc_v, func=ACT.Tanh)
             tanh_c[j] = th
             if j == js[-1]:
                 nc.sync.dma_start(out=out_c[:, :, js[0] * P:(js[-1] + 1) * P], in_=outs[js][1][:])
 
-        def ep2(j):
+        def ep_h(j, parts):
             js = group_of(j)
             off = (j - js[0]) * P
-            nc.vector.tensor_tensor(
-                out=outs[js][0][:, :, off:off + P], in0=banks[(j, "o")], in1=tanh_c[j][:], op=ALU.mult,
-            )
-            if j == js[-1]:
-                nc.sync.dma_start(out=out_h[:, :, js[0] * P:(js[-1] + 1) * P], in_=outs[js][0][:])
+            n = 4 // parts
+            for part in range(parts):
+                ts = slice(part * n, (part + 1) * n)
+                nc.vector.tensor_tensor(
+                    out=outs[js][0][:, ts, off:off + P], in0=banks[(j, "o")][:, ts, :], in1=tanh_c[j][:, ts, :],
+                    op=ALU.mult,
+                )
+                if j == js[-1]:
+                    nc.sync.dma_start(out=out_h[:, ts, js[0] * P:(js[-1] + 1) * P], in_=outs[js][0][:, ts, :])
 
-        for j in range(NT):
-            tr_w(j, 0)
-            tr_w(j, 1)
-            quant(j, 0)
-            tr_w(j, 2)
-            quant(j, 1)
-            tr_w(j, 3)
-            if j + AHEAD < NT:
-                load_weights(j + AHEAD)
-            if j >= 1:
-                tr_out(j - 1)
-            quant(j, 2)
-            if j >= 1:
-                ep1(j - 1)
-            quant(j, 3)
-            mx_act(j, 0)
-            mx_act(j, 1)
-            if j >= 1:
-                ep2(j - 1)
-            mul_ig(j)
-            mx_act(j, 2)
-            mx_act(j, 3)
-        tr_out(NT - 1)
-        ep1(NT - 1)
-        ep2(NT - 1)
+        tr_x(0, 0)
+        tr_x(0, 1)
+        tr_x(1, 0)
+        quant_x(0)
+        tr_x(1, 1)
+
+        bsum = const.tile([P, P], F32, name="bsum")
+        nc.vector.tensor_tensor(out=bsum[:], in0=braw[:, 0:P], in1=braw[:, P:2 * P], op=ALU.add)
+        pb = tr_pool.tile([P, 512], F32, name="pb", tag="tr")
+        nc.tensor.transpose(pb[:, 0:P], bsum[:], ident[:])
+        bias_sb = const.tile([P, 32], F32, name="bias_sb")
+        nc.vector.tensor_copy(out=bias_sb[:], in_=pb[:, 0:32])
+
+        tr_w(0)
+        quant_x(1)
+        quant(0)
+        for r in range(NR):
+            m = r // 2
+            if r + 1 < NR:
+                tr_w(r + 1)
+            if r % 2 == 0:
+                if m >= 1:
+                    tr_out(m - 1, "f")
+                    tr_out(m - 1, "u")
+                    ep_c(m - 1, 1)
+            else:
+                if m >= 1:
+                    tr_out(m - 1, "o")
+                    ep_h(m - 1, 1)
+                mul_ig(m)
+            if r + 1 < NR:
+                quant(r + 1)
+            mx_act(r, 0)
+            mx_act(r, 1)
+        tr_out(NT - 1, "f")
+        tr_out(NT - 1, "u")
+        tr_out(NT - 1, "o")
+        ep_c(NT - 1, TAIL_PARTS)
+        ep_h(NT - 1, TAIL_PARTS)

@@ -60,6 +60,16 @@ def tile_lstmcell_kernel(
         braw = const.tile([P, 2 * P], BF16, name="braw")
         nc.vector.memset(braw[:], 0.0)
 
+        zeros = const.tile([P, 512], BF16, name="zeros")
+        nc.vector.memset(zeros[:], 0.0)
+
+        def keep_clock(n, name):
+            idle = acc_pool.tile([P, 512], F32, name=name, tag="acc")
+            for i in range(n):
+                nc.tensor.matmul(out=idle[:], lhsT=zeros[:, 0:P], rhs=zeros[:], start=True, stop=True)
+
+        keep_clock(10, "idle_start")
+
         xraw = []
         for s, src in enumerate((x, h0)):
             xr = const.tile([P, 4 * K], BF16, name="xraw%d" % s)
@@ -153,7 +163,12 @@ def tile_lstmcell_kernel(
         def quant(r):
             wq[r] = code_pool.tile([P, 1024], U32, name="wq%d" % r, tag="wq", align_bytes=64)
             ws[r] = code_pool.tile([P, 1024], U8, name="ws%d" % r, tag="ws", align_bytes=64)
-            nc.vector.quantize_mx(out=wq[r][:].bitcast(FP8X4), scales=ws[r][:], in_=grp[r][:])
+            for hh in range(2):
+                nc.vector.quantize_mx(
+                    out=wq[r][:, hh * 512:(hh + 1) * 512].bitcast(FP8X4),
+                    scales=ws[r][:, hh * 512:(hh + 1) * 512],
+                    in_=grp[r][:, hh * 2048:(hh + 1) * 2048],
+                )
 
         def mx_act(r, hh):
             j = r // 2
@@ -235,10 +250,14 @@ def tile_lstmcell_kernel(
                     nc.sync.dma_start(out=out_h[:, ts, js[0] * P:(js[-1] + 1) * P], in_=outs[js][0][:, ts, :])
 
         tr_x(0, 0)
+        keep_clock(2, "idle_a")
         tr_x(0, 1)
+        keep_clock(2, "idle_b")
         tr_x(1, 0)
+        keep_clock(2, "idle_c")
         quant_x(0)
         tr_x(1, 1)
+        keep_clock(2, "idle_d")
 
         bsum = const.tile([P, P], F32, name="bsum")
         nc.vector.tensor_tensor(out=bsum[:], in0=braw[:, 0:P], in1=braw[:, P:2 * P], op=ALU.add)
@@ -248,6 +267,7 @@ def tile_lstmcell_kernel(
         nc.vector.tensor_copy(out=bias_sb[:], in_=pb[:, 0:32])
 
         tr_w(0)
+        keep_clock(2, "idle_e")
         quant_x(1)
         quant(0)
         for r in range(NR):

@@ -15,15 +15,13 @@ P = 128
 BATCH = 512
 K = 1024
 HID = 1024
-NT = HID // P
-NR = 2 * NT
+NPAIR = HID // (2 * P)
+NR = 4 * NPAIR
 FLOPS = 2 * BATCH * (2 * K) * (4 * HID)
 
 AHEAD = 10
-C0_AFTER = 3
-STORE_GROUPS = ((0, 1), (2, 3), (4, 5), (6,), (7,))
+C0_AFTER = 4
 W_EVAC_ON_SCALAR = (True, False, True, True)
-TAIL_PARTS = 2
 
 
 def tile_lstmcell_kernel(
@@ -37,7 +35,7 @@ def tile_lstmcell_kernel(
     nc = tc.nc
     weights = ((W_ii, W_hi), (W_ig, W_hg), (W_if, W_hf), (W_io, W_ho))
     biases = ((b_ii, b_hi), (b_ig, b_hg), (b_if, b_hf), (b_io, b_ho))
-    funcs = (ACT.Sigmoid, ACT.Tanh, ACT.Sigmoid, ACT.Sigmoid)
+    funcs = (ACT.Sigmoid, ACT.Tanh)
     out_h = out_0.rearrange("(p t) h -> p t h", t=4)
     out_c = out_1.rearrange("(p t) h -> p t h", t=4)
 
@@ -47,8 +45,7 @@ def tile_lstmcell_kernel(
         grp_pool = ctx.enter_context(tc.tile_pool(name="grp", bufs=3))
         code_pool = ctx.enter_context(tc.tile_pool(name="code", bufs=3))
         act_pool = ctx.enter_context(tc.tile_pool(name="act", bufs=2))
-        ep_pool = ctx.enter_context(tc.tile_pool(name="ep", bufs=2))
-        out_pool = ctx.enter_context(tc.tile_pool(name="outp", bufs=2))
+        ep_pool = ctx.enter_context(tc.tile_pool(name="ep", bufs=3))
         acc_pool = ctx.enter_context(tc.psum_pool(name="acc", bufs=2))
         tr_pool = ctx.enter_context(tc.psum_pool(name="tr", bufs=6))
         ctx.enter_context(tc.manual_schedule())
@@ -57,11 +54,14 @@ def tile_lstmcell_kernel(
         make_identity(nc, ident[:])
         warm = const.tile([P, 1], F32, name="warm")
         nc.vector.memset(warm[:], 0.0)
-        braw = const.tile([P, 2 * P], BF16, name="braw")
-        nc.vector.memset(braw[:], 0.0)
-
         zeros = const.tile([P, 512], BF16, name="zeros")
         nc.vector.memset(zeros[:], 0.0)
+        ones = const.tile([P, P], BF16, name="ones")
+        nc.vector.memset(ones[:], 1.0)
+        braw = const.tile([P, 2 * P], BF16, name="braw")
+        nc.vector.memset(braw[:], 0.0)
+        brow = const.tile([P, 2 * HID], BF16, name="brow")
+        nc.vector.memset(brow[:], 0.0)
 
         def keep_clock(n, name):
             idle = acc_pool.tile([P, 512], F32, name=name, tag="acc")
@@ -80,7 +80,13 @@ def tile_lstmcell_kernel(
                     in_=view[:, 2 * th:2 * th + 2, :],
                 )
             xraw.append(xr)
-        for q in range(4):
+        for q in range(2):
+            for s in range(2):
+                nc.scalar.dma_start(
+                    out=brow[s:s + 1, q * HID:(q + 1) * HID],
+                    in_=biases[2 + q][s].rearrange("(o n) -> o n", o=1),
+                )
+        for q in range(2):
             for s in range(2):
                 nc.scalar.dma_start(
                     out=braw[8 * q:8 * q + 8, s * P:(s + 1) * P],
@@ -93,12 +99,18 @@ def tile_lstmcell_kernel(
         wraw = {}
 
         def load_round(r):
-            j = r // 2
+            pair, k = divmod(r, 4)
             tiles = []
-            for hh in range(2):
-                for s in range(2):
-                    w = wraw_pool.tile([P, K], BF16, name="w%d_%d_%d" % (r, hh, s), tag="w")
-                    nc.sync.dma_start(out=w[:], in_=weights[2 * (r % 2) + hh][s][j * P:(j + 1) * P, :])
+            for a in range(2):
+                for b in range(2):
+                    if k < 2:
+                        src_w = weights[a][b]
+                        j = 2 * pair + k
+                    else:
+                        src_w = weights[k][a]
+                        j = 2 * pair + b
+                    w = wraw_pool.tile([P, K], BF16, name="w%d_%d_%d" % (r, a, b), tag="w")
+                    nc.sync.dma_start(out=w[:], in_=src_w[j * P:(j + 1) * P, :])
                     tiles.append(w)
             wraw[r] = tiles
             if r == C0_AFTER:
@@ -107,12 +119,11 @@ def tile_lstmcell_kernel(
         for r in range(AHEAD):
             load_round(r)
 
-        def transpose_bank(src32, cols, dst32, on_scalar, name):
+        def transpose_bank(src32, cols, dst, on_scalar, name):
             bank = tr_pool.tile([P, 512], F32, name=name, tag="tr")
             for i, c in enumerate(cols):
                 nc.tensor.transpose(bank[:, i * P:(i + 1) * P], src32[:, c:c + P], ident[:])
             src = bank[:].rearrange("p (a u c) -> p a c u", a=2, u=2)
-            dst = dst32.rearrange("p (a c u) -> p a c u", a=2, u=2)
             if on_scalar:
                 nc.scalar.copy(out=dst, in_=src)
             else:
@@ -131,7 +142,8 @@ def tile_lstmcell_kernel(
             for g in range(2):
                 cols = [(2 * th + tt) * 512 + 256 * g + 128 * u for tt in range(2) for u in range(2)]
                 base = g * 1024 + th * 512
-                transpose_bank(x32, cols, g32[:, base:base + 512], g == 0, "xb%d%d%d" % (s, th, g))
+                dst = g32[:, base:base + 512].rearrange("p (a c u) -> p a c u", a=2, u=2)
+                transpose_bank(x32, cols, dst, g == 0, "xb%d%d%d" % (s, th, g))
 
         def quant_x(s):
             nc.vector.quantize_mx(
@@ -145,17 +157,19 @@ def tile_lstmcell_kernel(
         ws = {}
         gate = {}
         prod = {}
-        banks = {}
-        outs = {}
+        back = {}
         tanh_c = {}
 
         def tr_w(r):
             grp[r] = grp_pool.tile([P, 4096], BF16, name="grp%d" % r, tag="grp", align_bytes=64)
             g32 = grp[r][:].bitcast(F32)
             for m in range(4):
+                if r % 4 < 2:
+                    dst = g32[:, m * 512:(m + 1) * 512].rearrange("p (a c u) -> p a c u", a=2, u=2)
+                else:
+                    dst = g32.rearrange("p (s a e c u) -> p s a e c u", s=2, a=2, e=2, u=2)[:, m // 2, :, m % 2, :, :]
                 transpose_bank(
-                    wraw[r][m][:].bitcast(F32), (0, 128, 256, 384), g32[:, m * 512:(m + 1) * 512],
-                    W_EVAC_ON_SCALAR[m], "wb%d_%d" % (r, m),
+                    wraw[r][m][:].bitcast(F32), (0, 128, 256, 384), dst, W_EVAC_ON_SCALAR[m], "wb%d_%d" % (r, m),
                 )
             if r + AHEAD < NR:
                 load_round(r + AHEAD)
@@ -170,126 +184,151 @@ def tile_lstmcell_kernel(
                     in_=grp[r][:, hh * 2048:(hh + 1) * 2048],
                 )
 
-        def mx_act(r, hh):
-            j = r // 2
-            q = 2 * (r % 2) + hh
-            acc = acc_pool.tile([P, 512], F32, name="acc%d_%d" % (j, q), tag="acc")
-            for s in range(2):
-                for g in range(2):
-                    wc = (2 * hh + s) * 256 + g * 128
-                    xc = (2 * s + g) * 512
-                    nc.tensor.matmul_mx(
-                        out=acc[:],
-                        lhsT=wq[r][:, wc:wc + 128].bitcast(FP8X4),
-                        lhsT_scale=ws[r][:, wc:wc + 128],
-                        rhs=xq[:, xc:xc + 512].bitcast(FP8X4),
-                        rhs_scale=xs[:, xc:xc + 512],
-                        start=(s == 0 and g == 0),
-                        stop=(s == 1 and g == 1),
-                    )
-            a = act_pool.tile([P, 512], F32, name="gate%d_%d" % (j, q), tag="gate%d" % q)
-            nc.scalar.activation(
-                out=a[:], in_=acc[:], func=funcs[q],
-                bias=bias_sb[:, 8 * q + j:8 * q + j + 1], scale=1.0,
-            )
-            gate[(j, q)] = a
+        def mx_weights_stationary(r):
+            pair, k = divmod(r, 4)
+            j = 2 * pair + k
+            for q in range(2):
+                acc = acc_pool.tile([P, 512], F32, name="acc%d_%d" % (r, q), tag="acc")
+                for s in range(2):
+                    for g in range(2):
+                        wc = (2 * q + s) * 256 + g * 128
+                        xc = (2 * s + g) * 512
+                        nc.tensor.matmul_mx(
+                            out=acc[:],
+                            lhsT=wq[r][:, wc:wc + 128].bitcast(FP8X4),
+                            lhsT_scale=ws[r][:, wc:wc + 128],
+                            rhs=xq[:, xc:xc + 512].bitcast(FP8X4),
+                            rhs_scale=xs[:, xc:xc + 512],
+                            start=(s == 0 and g == 0),
+                            stop=(s == 1 and g == 1),
+                        )
+                a = act_pool.tile([P, 512], F32, name="gate%d_%d" % (j, q), tag="gate%d" % q)
+                nc.scalar.activation(
+                    out=a[:], in_=acc[:], func=funcs[q],
+                    bias=bias_sb[:, 8 * q + j:8 * q + j + 1], scale=1.0,
+                )
+                gate[(j, q)] = a
+
+        def mx_batch_stationary(r):
+            pair, k = divmod(r, 4)
+            bias = bias_bc[:, (k - 2) * HID + pair * 256:(k - 2) * HID + (pair + 1) * 256]
+            for tp in range(2):
+                acc = acc_pool.tile([P, 512], F32, name="acc%d_%d" % (r, tp), tag="acc")
+                for tt in range(2):
+                    for s in range(2):
+                        for g in range(2):
+                            xc = (2 * s + g) * 512 + (2 * tp + tt) * 128
+                            wc = s * 512 + g * 256
+                            nc.tensor.matmul_mx(
+                                out=acc[:, tt * 256:(tt + 1) * 256],
+                                lhsT=xq[:, xc:xc + 128].bitcast(FP8X4),
+                                lhsT_scale=xs[:, xc:xc + 128],
+                                rhs=wq[r][:, wc:wc + 256].bitcast(FP8X4),
+                                rhs_scale=ws[r][:, wc:wc + 256],
+                                start=(s == 0 and g == 0),
+                                stop=(s == 1 and g == 1),
+                            )
+                a = ep_pool.tile([P, 2, 256], F32, name="fo%d_%d" % (r, tp), tag="fo%d" % k)
+                nc.vector.tensor_tensor(
+                    out=a[:], in0=acc[:].rearrange("p (t c) -> p t c", t=2),
+                    in1=bias.unsqueeze(1).to_broadcast([P, 2, 256]), op=ALU.add,
+                )
+                nc.scalar.activation(out=a[:], in_=a[:], func=ACT.Sigmoid)
+                gate[(pair, k, tp)] = a
 
         def mul_ig(j):
-            t = act_pool.tile([P, 512], F32, name="ig%d" % j, tag="ig")
+            t = ep_pool.tile([P, 512], F32, name="ig%d" % j, tag="ig")
             nc.vector.tensor_tensor(out=t[:], in0=gate[(j, 0)][:], in1=gate[(j, 1)][:], op=ALU.mult)
             prod[j] = t
 
-        def tr_out(j, key):
-            src = {"f": gate[(j, 2)], "u": prod[j], "o": gate[(j, 3)]}[key]
-            bank = tr_pool.tile([P, 512], F32, name="ob%s%d" % (key, j), tag="tr")
-            for t in range(4):
-                nc.tensor.transpose(bank[:, t * P:(t + 1) * P], src[:, t * P:(t + 1) * P], ident[:])
-            banks[(j, key)] = bank[:].rearrange("p (t h) -> p t h", t=4)
+        def tr_back(pair, tp):
+            bank = tr_pool.tile([P, 512], F32, name="ob%d_%d" % (pair, tp), tag="tr")
+            for tt in range(2):
+                for e in range(2):
+                    t = 2 * tp + tt
+                    nc.tensor.transpose(
+                        bank[:, (2 * tt + e) * P:(2 * tt + e + 1) * P], prod[2 * pair + e][:, t * P:(t + 1) * P], ident[:],
+                    )
+            back[(pair, tp)] = bank[:].rearrange("p (t c) -> p t c", t=2)
 
-        def group_of(j):
-            for grp_js in STORE_GROUPS:
-                if j in grp_js:
-                    return grp_js
-            return None
+        def ep_c(pair, tp):
+            ts = slice(2 * tp, 2 * tp + 2)
+            hs = slice(pair * 256, (pair + 1) * 256)
+            t1 = ep_pool.tile([P, 2, 256], F32, name="t1_%d_%d" % (pair, tp), tag="t1")
+            nc.vector.tensor_tensor(out=t1[:], in0=gate[(pair, 2, tp)][:], in1=c0_v[:, ts, hs], op=ALU.mult)
+            oc = ep_pool.tile([P, 2, 256], F32, name="oc%d_%d" % (pair, tp), tag="oc")
+            nc.vector.tensor_tensor(out=oc[:], in0=back[(pair, tp)], in1=t1[:], op=ALU.add)
+            th = ep_pool.tile([P, 2, 256], F32, name="th%d_%d" % (pair, tp), tag="th")
+            nc.scalar.activation(out=th[:], in_=oc[:], func=ACT.Tanh)
+            tanh_c[(pair, tp)] = th
+            nc.sync.dma_start(out=out_c[:, ts, hs], in_=oc[:])
 
-        def ep_c(j, parts):
-            js = group_of(j)
-            width = P * len(js)
-            if j == js[0]:
-                outs[js] = (
-                    out_pool.tile([P, 4, width], F32, name="oh%d" % j, tag="oh"),
-                    out_pool.tile([P, 4, width], F32, name="oc%d" % j, tag="oc"),
-                )
-            off = (j - js[0]) * P
-            t1 = ep_pool.tile([P, 4, P], F32, name="t1_%d" % j, tag="t1")
-            th = ep_pool.tile([P, 4, P], F32, name="th%d" % j, tag="th")
-            n = 4 // parts
-            for part in range(parts):
-                ts = slice(part * n, (part + 1) * n)
-                oc_v = outs[js][1][:, ts, off:off + P]
-                nc.vector.tensor_tensor(
-                    out=t1[:, ts, :], in0=banks[(j, "f")][:, ts, :], in1=c0_v[:, ts, j * P:(j + 1) * P], op=ALU.mult,
-                )
-                nc.vector.tensor_tensor(out=oc_v, in0=banks[(j, "u")][:, ts, :], in1=t1[:, ts, :], op=ALU.add)
-                nc.scalar.activation(out=th[:, ts, :], in_=oc_v, func=ACT.Tanh)
-            tanh_c[j] = th
-            if j == js[-1]:
-                nc.sync.dma_start(out=out_c[:, :, js[0] * P:(js[-1] + 1) * P], in_=outs[js][1][:])
+        def ep_h(pair, tp):
+            ts = slice(2 * tp, 2 * tp + 2)
+            hs = slice(pair * 256, (pair + 1) * 256)
+            oh = ep_pool.tile([P, 2, 256], F32, name="oh%d_%d" % (pair, tp), tag="oh")
+            nc.vector.tensor_tensor(out=oh[:], in0=gate[(pair, 3, tp)][:], in1=tanh_c[(pair, tp)][:], op=ALU.mult)
+            nc.sync.dma_start(out=out_h[:, ts, hs], in_=oh[:])
 
-        def ep_h(j, parts):
-            js = group_of(j)
-            off = (j - js[0]) * P
-            n = 4 // parts
-            for part in range(parts):
-                ts = slice(part * n, (part + 1) * n)
-                nc.vector.tensor_tensor(
-                    out=outs[js][0][:, ts, off:off + P], in0=banks[(j, "o")][:, ts, :], in1=tanh_c[j][:, ts, :],
-                    op=ALU.mult,
-                )
-                if j == js[-1]:
-                    nc.sync.dma_start(out=out_h[:, ts, js[0] * P:(js[-1] + 1) * P], in_=outs[js][0][:, ts, :])
+        bias_bc = const.tile([P, 2 * HID], F32, name="bias_bc")
+
+        def spread_bias(n):
+            pbc = tr_pool.tile([P, 512], F32, name="pbc%d" % n, tag="tr")
+            nc.tensor.matmul(out=pbc[:], lhsT=ones[:], rhs=brow[:, n * 512:(n + 1) * 512], start=True, stop=True)
+            nc.scalar.copy(out=bias_bc[:, n * 512:(n + 1) * 512], in_=pbc[:])
 
         tr_x(0, 0)
         keep_clock(2, "idle_a")
         tr_x(0, 1)
         keep_clock(2, "idle_b")
         tr_x(1, 0)
-        keep_clock(2, "idle_c")
+        spread_bias(0)
+        spread_bias(1)
         quant_x(0)
         tr_x(1, 1)
-        keep_clock(2, "idle_d")
+        spread_bias(2)
+        spread_bias(3)
 
         bsum = const.tile([P, P], F32, name="bsum")
         nc.vector.tensor_tensor(out=bsum[:], in0=braw[:, 0:P], in1=braw[:, P:2 * P], op=ALU.add)
         pb = tr_pool.tile([P, 512], F32, name="pb", tag="tr")
         nc.tensor.transpose(pb[:, 0:P], bsum[:], ident[:])
-        bias_sb = const.tile([P, 32], F32, name="bias_sb")
-        nc.vector.tensor_copy(out=bias_sb[:], in_=pb[:, 0:32])
+        bias_sb = const.tile([P, 16], F32, name="bias_sb")
+        nc.vector.tensor_copy(out=bias_sb[:], in_=pb[:, 0:16])
 
         tr_w(0)
         keep_clock(2, "idle_e")
         quant_x(1)
         quant(0)
         for r in range(NR):
-            m = r // 2
+            pair, k = divmod(r, 4)
+            last = pair == NPAIR - 1
             if r + 1 < NR:
                 tr_w(r + 1)
-            if r % 2 == 0:
-                if m >= 1:
-                    tr_out(m - 1, "f")
-                    tr_out(m - 1, "u")
-                    ep_c(m - 1, 1)
-            else:
-                if m >= 1:
-                    tr_out(m - 1, "o")
-                    ep_h(m - 1, 1)
-                mul_ig(m)
+            if k == 3:
+                tr_back(pair, 0)
+                if last:
+                    tr_back(pair, 1)
+            if k == 0 and pair >= 1:
+                tr_back(pair - 1, 1)
+            if k == 1:
+                if pair >= 1:
+                    ep_h(pair - 1, 0)
+                    ep_h(pair - 1, 1)
+                mul_ig(2 * pair)
+            if k == 2:
+                mul_ig(2 * pair + 1)
+            if k == 3:
+                ep_c(pair, 0)
+                if last:
+                    ep_c(pair, 1)
+            if k == 0 and pair >= 1:
+                ep_c(pair - 1, 1)
             if r + 1 < NR:
                 quant(r + 1)
-            mx_act(r, 0)
-            mx_act(r, 1)
-        tr_out(NT - 1, "f")
-        tr_out(NT - 1, "u")
-        tr_out(NT - 1, "o")
-        ep_c(NT - 1, TAIL_PARTS)
-        ep_h(NT - 1, TAIL_PARTS)
+            if k < 2:
+                mx_weights_stationary(r)
+            else:
+                mx_batch_stationary(r)
+        ep_h(NPAIR - 1, 0)
+        ep_h(NPAIR - 1, 1)

@@ -238,7 +238,7 @@ def tile_lstmcell_kernel(
 
         def mul_ig(j):
             t = ep_pool.tile([P, 512], F32, name="ig%d" % j, tag="ig")
-            nc.vector.tensor_tensor(out=t[:], in0=gate[(j, 0)][:], in1=gate[(j, 1)][:], op=ALU.mult)
+            nc.gpsimd.tensor_tensor(out=t[:], in0=gate[(j, 0)][:], in1=gate[(j, 1)][:], op=ALU.mult)
             prod[j] = t
 
         def tr_back(pair, tp):
@@ -255,7 +255,7 @@ def tile_lstmcell_kernel(
             ts = slice(2 * tp, 2 * tp + 2)
             hs = slice(pair * 256, (pair + 1) * 256)
             t1 = ep_pool.tile([P, 2, 256], F32, name="t1_%d_%d" % (pair, tp), tag="t1")
-            nc.vector.tensor_tensor(out=t1[:], in0=gate[(pair, 2, tp)][:], in1=c0_v[:, ts, hs], op=ALU.mult)
+            nc.gpsimd.tensor_tensor(out=t1[:], in0=gate[(pair, 2, tp)][:], in1=c0_v[:, ts, hs], op=ALU.mult)
             oc = ep_pool.tile([P, 2, 256], F32, name="oc%d_%d" % (pair, tp), tag="oc")
             nc.vector.tensor_tensor(out=oc[:], in0=back[(pair, tp)], in1=t1[:], op=ALU.add)
             th = ep_pool.tile([P, 2, 256], F32, name="th%d_%d" % (pair, tp), tag="th")

from contextlib import ExitStack

import concourse.mybir as mybir
from concourse.masks import make_identity

F32 = mybir.dt.float32
BF16 = mybir.dt.bfloat16
U32 = mybir.dt.uint32
U8 = mybir.dt.uint8
FP8X4 = mybir.dt.float8_e4m3fn_x4
ACT = mybir.ActivationFunctionType
ALU = mybir.AluOpType

P = 128
BATCH = 512
K = 1024
HID = 1024
NPAIR = HID // (2 * P)
NR = 4 * NPAIR
FLOPS = 2 * BATCH * (2 * K) * (4 * HID)

AHEAD = 10
C0_AFTER = 4
W_EVAC_ON_SCALAR = (True, False, True, True)


def tile_lstmcell_kernel(
    tc, x, h0, c0,
    W_ii, b_ii, W_hi, b_hi,
    W_if, b_if, W_hf, b_hf,
    W_ig, b_ig, W_hg, b_hg,
    W_io, b_io, W_ho, b_ho,
    out_0, out_1,
):
    nc = tc.nc
    weights = ((W_ii, W_hi), (W_ig, W_hg), (W_if, W_hf), (W_io, W_ho))
    biases = ((b_ii, b_hi), (b_ig, b_hg), (b_if, b_hf), (b_io, b_ho))
    funcs = (ACT.Sigmoid, ACT.Tanh)
    out_h = out_0.rearrange("(p t) h -> p t h", t=4)
    out_c = out_1.rearrange("(p t) h -> p t h", t=4)

    with ExitStack() as ctx:
        const = ctx.enter_context(tc.tile_pool(name="const", bufs=1))
        wraw_pool = ctx.enter_context(tc.tile_pool(name="wraw", bufs=4 * AHEAD))
        grp_pool = ctx.enter_context(tc.tile_pool(name="grp", bufs=3))
        code_pool = ctx.enter_context(tc.tile_pool(name="code", bufs=3))
        act_pool = ctx.enter_context(tc.tile_pool(name="act", bufs=2))
        ep_pool = ctx.enter_context(tc.tile_pool(name="ep", bufs=3))
        acc_pool = ctx.enter_context(tc.psum_pool(name="acc", bufs=2))
        tr_pool = ctx.enter_context(tc.psum_pool(name="tr", bufs=6))
        ctx.enter_context(tc.manual_schedule())

        ident = const.tile([P, P], F32, name="ident")
        make_identity(nc, ident[:])
        warm = const.tile([P, 1], F32, name="warm")
        nc.vector.memset(warm[:], 0.0)
        zeros = const.tile([P, 512], BF16, name="zeros")
        nc.vector.memset(zeros[:], 0.0)
        ones = const.tile([P, P], BF16, name="ones")
        nc.vector.memset(ones[:], 1.0)
        braw = const.tile([P, 2 * P], BF16, name="braw")
        nc.vector.memset(braw[:], 0.0)
        brow = const.tile([P, 2 * HID], BF16, name="brow")
        nc.vector.memset(brow[:], 0.0)

        def keep_clock(n, name):
            idle = acc_pool.tile([P, 512], F32, name=name, tag="acc")
            for i in range(n):
                nc.tensor.matmul(out=idle[:], lhsT=zeros[:, 0:P], rhs=zeros[:], start=True, stop=True)

        keep_clock(10, "idle_start")

        xraw = []
        for s, src in enumerate((x, h0)):
            xr = const.tile([P, 4 * K], BF16, name="xraw%d" % s)
            view = src.rearrange("(p t) k -> p t k", t=4)
            for th in range(2):
                nc.sync.dma_start(
                    out=xr[:, th * 2 * K:(th + 1) * 2 * K].rearrange("p (t k) -> p t k", t=2),
                    in_=view[:, 2 * th:2 * th + 2, :],
                )
            xraw.append(xr)
        for q in range(2):
            for s in range(2):
                nc.scalar.dma_start(
                    out=brow[s:s + 1, q * HID:(q + 1) * HID],
                    in_=biases[2 + q][s].rearrange("(o n) -> o n", o=1),
                )
        for q in range(2):
            for s in range(2):
                nc.scalar.dma_start(
                    out=braw[8 * q:8 * q + 8, s * P:(s + 1) * P],
                    in_=biases[q][s].rearrange("(j p) -> j p", p=P),
                )
        nc.scalar.activation(out=warm[:], in_=warm[:], func=ACT.Sigmoid)

        c0_sb = const.tile([P, 4 * HID], BF16, name="c0_sb")
        c0_v = c0_sb[:].rearrange("p (t h) -> p t h", t=4)
        wraw = {}

        def load_round(r):
            pair, k = divmod(r, 4)
            tiles = []
            for a in range(2):
                for b in range(2):
                    if k < 2:
                        src_w = weights[a][b]
                        j = 2 * pair + k
                    else:
                        src_w = weights[k][a]
                        j = 2 * pair + b
                    w = wraw_pool.tile([P, K], BF16, name="w%d_%d_%d" % (r, a, b), tag="w")
                    nc.sync.dma_start(out=w[:], in_=src_w[j * P:(j + 1) * P, :])
                    tiles.append(w)
            wraw[r] = tiles
            if r == C0_AFTER:
                nc.sync.dma_start(out=c0_sb[:], in_=c0.rearrange("(p t) h -> p (t h)", t=4))

        for r in range(AHEAD):
            load_round(r)

        def transpose_bank(src32, cols, dst, on_scalar, name):
            bank = tr_pool.tile([P, 512], F32, name=name, tag="tr")
            for i, c in enumerate(cols):
                nc.tensor.transpose(bank[:, i * P:(i + 1) * P], src32[:, c:c + P], ident[:])
            src = bank[:].rearrange("p (a u c) -> p a c u", a=2, u=2)
            if on_scalar:
                nc.scalar.copy(out=dst, in_=src)
            else:
                nc.vector.tensor_copy(out=dst, in_=src)

        xq = const.tile([P, 4 * 512], U32, name="xq", align_bytes=64)
        xs = const.tile([P, 4 * 512], U8, name="xs", align_bytes=64)
        xgrp = []
        for s in range(2):
            xg = grp_pool.tile([P, 4096], BF16, name="xgrp%d" % s, tag="grp", align_bytes=64)
            xgrp.append(xg)

        def tr_x(s, th):
            x32 = xraw[s][:].bitcast(F32)
            g32 = xgrp[s][:].bitcast(F32)
            for g in range(2):
                cols = [(2 * th + tt) * 512 + 256 * g + 128 * u for tt in range(2) for u in range(2)]
                base = g * 1024 + th * 512
                dst = g32[:, base:base + 512].rearrange("p (a c u) -> p a c u", a=2, u=2)
                transpose_bank(x32, cols, dst, g == 0, "xb%d%d%d" % (s, th, g))

        def quant_x(s):
            nc.vector.quantize_mx(
                out=xq[:, s * 1024:(s + 1) * 1024].bitcast(FP8X4),
                scales=xs[:, s * 1024:(s + 1) * 1024],
                in_=xgrp[s][:],
            )

        grp = {}
        wq = {}
        ws = {}
        gate = {}
        prod = {}
        back = {}
        tanh_c = {}

        def tr_w(r):
            grp[r] = grp_pool.tile([P, 4096], BF16, name="grp%d" % r, tag="grp", align_bytes=64)
            g32 = grp[r][:].bitcast(F32)
            for m in range(4):
                if r % 4 < 2:
                    dst = g32[:, m * 512:(m + 1) * 512].rearrange("p (a c u) -> p a c u", a=2, u=2)
                else:
                    dst = g32.rearrange("p (s a e c u) -> p s a e c u", s=2, a=2, e=2, u=2)[:, m // 2, :, m % 2, :, :]
                transpose_bank(
                    wraw[r][m][:].bitcast(F32), (0, 128, 256, 384), dst, W_EVAC_ON_SCALAR[m], "wb%d_%d" % (r, m),
                )
            if r + AHEAD < NR:
                load_round(r + AHEAD)

        def quant(r):
            wq[r] = code_pool.tile([P, 1024], U32, name="wq%d" % r, tag="wq", align_bytes=64)
            ws[r] = code_pool.tile([P, 1024], U8, name="ws%d" % r, tag="ws", align_bytes=64)
            for hh in range(2):
                nc.vector.quantize_mx(
                    out=wq[r][:, hh * 512:(hh + 1) * 512].bitcast(FP8X4),
                    scales=ws[r][:, hh * 512:(hh + 1) * 512],
                    in_=grp[r][:, hh * 2048:(hh + 1) * 2048],
                )

        def mx_weights_stationary(r):
            pair, k = divmod(r, 4)
            j = 2 * pair + k
            for q in range(2):
                acc = acc_pool.tile([P, 512], F32, name="acc%d_%d" % (r, q), tag="acc")
                for s in range(2):
                    for g in range(2):
                        wc = (2 * q + s) * 256 + g * 128
                        xc = (2 * s + g) * 512
                        nc.tensor.matmul_mx(
                            out=acc[:],
                            lhsT=wq[r][:, wc:wc + 128].bitcast(FP8X4),
                            lhsT_scale=ws[r][:, wc:wc + 128],
                            rhs=xq[:, xc:xc + 512].bitcast(FP8X4),
                            rhs_scale=xs[:, xc:xc + 512],
                            start=(s == 0 and g == 0),
                            stop=(s == 1 and g == 1),
                        )
                a = act_pool.tile([P, 512], F32, name="gate%d_%d" % (j, q), tag="gate%d" % q)
                nc.scalar.activation(
                    out=a[:], in_=acc[:], func=funcs[q],
                    bias=bias_sb[:, 8 * q + j:8 * q + j + 1], scale=1.0,
                )
                gate[(j, q)] = a

        def mx_batch_stationary(r):
            pair, k = divmod(r, 4)
            bias = bias_bc[:, (k - 2) * HID + pair * 256:(k - 2) * HID + (pair + 1) * 256]
            for tp in range(2):
                acc = acc_pool.tile([P, 512], F32, name="acc%d_%d" % (r, tp), tag="acc")
                for tt in range(2):
                    for s in range(2):
                        for g in range(2):
                            xc = (2 * s + g) * 512 + (2 * tp + tt) * 128
                            wc = s * 512 + g * 256
                            nc.tensor.matmul_mx(
                                out=acc[:, tt * 256:(tt + 1) * 256],
                                lhsT=xq[:, xc:xc + 128].bitcast(FP8X4),
                                lhsT_scale=xs[:, xc:xc + 128],
                                rhs=wq[r][:, wc:wc + 256].bitcast(FP8X4),
                                rhs_scale=ws[r][:, wc:wc + 256],
                                start=(s == 0 and g == 0),
                                stop=(s == 1 and g == 1),
                            )
                a = ep_pool.tile([P, 2, 256], F32, name="fo%d_%d" % (r, tp), tag="fo%d" % k)
                nc.vector.tensor_tensor(
                    out=a[:], in0=acc[:].rearrange("p (t c) -> p t c", t=2),
                    in1=bias.unsqueeze(1).to_broadcast([P, 2, 256]), op=ALU.add,
                )
                nc.scalar.activation(out=a[:], in_=a[:], func=ACT.Sigmoid)
                gate[(pair, k, tp)] = a

        def mul_ig(j):
            t = ep_pool.tile([P, 512], F32, name="ig%d" % j, tag="ig")
            nc.gpsimd.tensor_tensor(out=t[:], in0=gate[(j, 0)][:], in1=gate[(j, 1)][:], op=ALU.mult)
            prod[j] = t

        def tr_back(pair, tp):
            bank = tr_pool.tile([P, 512], F32, name="ob%d_%d" % (pair, tp), tag="tr")
            for tt in range(2):
                for e in range(2):
                    t = 2 * tp + tt
                    nc.tensor.transpose(
                        bank[:, (2 * tt + e) * P:(2 * tt + e + 1) * P], prod[2 * pair + e][:, t * P:(t + 1) * P], ident[:],
                    )
            back[(pair, tp)] = bank[:].rearrange("p (t c) -> p t c", t=2)

        def ep_c(pair, tp):
            ts = slice(2 * tp, 2 * tp + 2)
            hs = slice(pair * 256, (pair + 1) * 256)
            t1 = ep_pool.tile([P, 2, 256], F32, name="t1_%d_%d" % (pair, tp), tag="t1")
            nc.gpsimd.tensor_tensor(out=t1[:], in0=gate[(pair, 2, tp)][:], in1=c0_v[:, ts, hs], op=ALU.mult)
            oc = ep_pool.tile([P, 2, 256], F32, name="oc%d_%d" % (pair, tp), tag="oc")
            nc.vector.tensor_tensor(out=oc[:], in0=back[(pair, tp)], in1=t1[:], op=ALU.add)
            th = ep_pool.tile([P, 2, 256], F32, name="th%d_%d" % (pair, tp), tag="th")
            nc.scalar.activation(out=th[:], in_=oc[:], func=ACT.Tanh)
            tanh_c[(pair, tp)] = th
            nc.sync.dma_start(out=out_c[:, ts, hs], in_=oc[:])

        def ep_h(pair, tp):
            ts = slice(2 * tp, 2 * tp + 2)
            hs = slice(pair * 256, (pair + 1) * 256)
            oh = ep_pool.tile([P, 2, 256], F32, name="oh%d_%d" % (pair, tp), tag="oh")
            nc.vector.tensor_tensor(out=oh[:], in0=gate[(pair, 3, tp)][:], in1=tanh_c[(pair, tp)][:], op=ALU.mult)
            nc.sync.dma_start(out=out_h[:, ts, hs], in_=oh[:])

        bias_bc = const.tile([P, 2 * HID], F32, name="bias_bc")

        def spread_bias(n):
            pbc = tr_pool.tile([P, 512], F32, name="pbc%d" % n, tag="tr")
            nc.tensor.matmul(out=pbc[:], lhsT=ones[:], rhs=brow[:, n * 512:(n + 1) * 512], start=True, stop=True)
            nc.scalar.copy(out=bias_bc[:, n * 512:(n + 1) * 512], in_=pbc[:])

        tr_x(0, 0)
        keep_clock(2, "idle_a")
        tr_x(0, 1)
        keep_clock(2, "idle_b")
        tr_x(1, 0)
        spread_bias(0)
        spread_bias(1)
        quant_x(0)
        tr_x(1, 1)
        spread_bias(2)
        spread_bias(3)

        bsum = const.tile([P, P], F32, name="bsum")
        nc.vector.tensor_tensor(out=bsum[:], in0=braw[:, 0:P], in1=braw[:, P:2 * P], op=ALU.add)
        pb = tr_pool.tile([P, 512], F32, name="pb", tag="tr")
        nc.tensor.transpose(pb[:, 0:P], bsum[:], ident[:])
        bias_sb = const.tile([P, 16], F32, name="bias_sb")
        nc.vector.tensor_copy(out=bias_sb[:], in_=pb[:, 0:16])

        tr_w(0)
        keep_clock(2, "idle_e")
        quant_x(1)
        quant(0)
        for r in range(NR):
            pair, k = divmod(r, 4)
            last = pair == NPAIR - 1
            if r + 1 < NR:
                tr_w(r + 1)
            if k == 3:
                tr_back(pair, 0)
                if last:
                    tr_back(pair, 1)
            if k == 0 and pair >= 1:
                tr_back(pair - 1, 1)
            if k == 1:
                if pair >= 1:
                    ep_h(pair - 1, 0)
                    ep_h(pair - 1, 1)
                mul_ig(2 * pair)
            if k == 2:
                mul_ig(2 * pair + 1)
            if k == 3:
                ep_c(pair, 0)
                if last:
                    ep_c(pair, 1)
            if k == 0 and pair >= 1:
                ep_c(pair - 1, 1)
            if r + 1 < NR:
                quant(r + 1)
            if k < 2:
                mx_weights_stationary(r)
            else:
                mx_batch_stationary(r)
        ep_h(NPAIR - 1, 0)
        ep_h(NPAIR - 1, 1)
